import numpy as np
import ml_dtypes


def mxq(x, axis, fmt="e4m3"):
    dtype, down = {"e4m3": (ml_dtypes.float8_e4m3fn, 7), "e5m2": (ml_dtypes.float8_e5m2, 14)}[fmt]
    v = np.moveaxis(np.asarray(x, np.float32).astype(ml_dtypes.bfloat16).astype(np.float64), axis, -1)
    blocks = v.reshape(v.shape[:-1] + (-1, 32))
    amax = np.abs(blocks).max(-1, keepdims=True)
    byte = np.maximum(np.where(amax > 0, np.frexp(amax)[1] - 1 + 127, 0) - down, 1)
    scale = np.exp2(byte - 127.0)
    codes = (blocks / scale).astype(np.float32).astype(dtype).astype(np.float64)
    return np.moveaxis((codes * scale).reshape(v.shape), -1, axis)


WIDE = False


def mx_kscale(k):
    if not WIDE:
        return np.ones(k)
    levels = np.array([10, -10, 5, -5, 0])
    a = np.random.permutation(np.resize(levels, k // 512 * 4)).reshape(k // 512, 4)
    idx = np.arange(k)
    return np.exp2(a[idx // 512, idx % 128 // 32])


BF16 = ml_dtypes.bfloat16


def bf(x):
    return np.asarray(x, np.float32).astype(BF16)


def f64(x):
    return np.asarray(x).astype(np.float64)


E2M1 = np.array([0.0, 0.5, 1.0, 1.5, 2.0, 3.0, 4.0, 6.0, -0.0, -0.5, -1.0, -1.5, -2.0, -3.0, -4.0, -6.0])


def pack_weight(w, fmt):
    k, n = w.shape
    w = f64(bf(w)).reshape(k // 32, 32, n)
    amax = np.abs(w).max(1)
    if fmt == "e4m3":
        byte = np.frexp(amax)[1] - 1 + 127 - 7
    else:
        mant, ex = np.frexp(amax / 6.0)
        byte = np.where(mant > 0.5, ex, ex - 1) + 127
    byte = np.clip(np.where(amax > 0, byte, 1), 1, 254)
    scaled = (w * np.exp2(127.0 - byte)[:, None, :]).reshape(k, n).astype(np.float32)
    by_word = np.ascontiguousarray(scaled.reshape(k // 512, 128, 4, n).transpose(0, 1, 3, 2))
    if fmt == "e4m3":
        words = by_word.astype(ml_dtypes.float8_e4m3fn).view(np.uint8)
    else:
        c = by_word.astype(ml_dtypes.float4_e2m1fn).view(np.uint8) & 0xF
        words = c[..., 0::2] | (c[..., 1::2] << 4)
    return np.ascontiguousarray(words), np.ascontiguousarray(byte.astype(np.uint8).reshape(k // 512, 16, n))


def unpack_weight(words, scales, fmt):
    g, p, n, _ = words.shape
    if fmt == "e4m3":
        vals = np.ascontiguousarray(words).view(ml_dtypes.float8_e4m3fn).astype(np.float64)
    else:
        nib = np.empty((g, p, n, 4), np.uint8)
        nib[..., 0::2] = words & 0xF
        nib[..., 1::2] = words >> 4
        vals = E2M1[nib]
    vals = vals * np.repeat(np.exp2(scales.astype(np.float64) - 127.0), 8, axis=1)[..., None]
    return vals.transpose(0, 1, 3, 2).reshape(g * 512, n)


N, C, T, V, IC = 1, 16384, 2, 128, 512
G = (IC * T) ** 0.25


def setup_inputs():
    s = mx_kscale(C)
    u = mx_kscale(IC * T)[::T]
    x = bf(np.random.standard_normal((N, C, T, V)) * s[None, :, None, None])
    Wa = np.random.standard_normal((IC, C)) * G / np.sqrt(C) / s[None, :] * u[:, None]
    Wa_words, Wa_scales = pack_weight(Wa.T, "e4m3")
    ba = bf(np.random.standard_normal(IC) * 0.3 * G * u)
    Wb = np.random.standard_normal((IC, C)) * G / np.sqrt(C) / s[None, :] / u[:, None]
    Wb_words, Wb_scales = pack_weight(Wb.T, "e4m3")
    bb = bf(np.random.standard_normal(IC) * 0.3 * G / u)
    A = bf(np.eye(V)[None] + 0.1 * np.random.standard_normal((1, V, V)))
    alpha = bf(2.0 + 0.2 * np.random.standard_normal(1))
    return {"x": x,
            "Wa_words": Wa_words,
            "Wa_scales": Wa_scales,
            "ba": ba,
            "Wb_words": Wb_words,
            "Wb_scales": Wb_scales,
            "bb": bb,
            "A": A,
            "alpha": alpha}


def reference(x, Wa_words, Wa_scales, ba, Wb_words, Wb_scales, bb, A, alpha):
    n, c, t, v = x.shape
    wa = unpack_weight(Wa_words, Wa_scales, "e4m3").T
    wb = unpack_weight(Wb_words, Wb_scales, "e4m3").T
    ic = wa.shape[0]
    xq = mxq(f64(x), 1, "e4m3").reshape(n, c, t * v)
    qa = (wa @ xq).reshape(n, ic, t, v) + f64(ba)[None, :, None, None]
    kb = (wb @ xq).reshape(n, ic, t, v) + f64(bb)[None, :, None, None]
    Q = qa.transpose(0, 3, 1, 2).reshape(n, v, ic * t)
    K = kb.reshape(n, ic * t, v)
    Graph_B = np.tanh((mxq(Q, 2, "e4m3") @ mxq(K, 1, "e4m3")) / (ic * t))
    z = f64(A) + Graph_B * f64(alpha)
    e = np.exp(z - z.max(-1, keepdims=True))
    return e / e.sum(-1, keepdims=True)

@@ -1,0 +1,221 @@
+from contextlib import ExitStack
+
+import concourse.mybir as mybir
+from concourse.masks import make_identity
+
+F32 = mybir.dt.float32
+BF16 = mybir.dt.bfloat16
+I32 = mybir.dt.int32
+U32 = mybir.dt.uint32
+U8 = mybir.dt.uint8
+FP8X4 = mybir.dt.float8_e4m3fn_x4
+ACT = mybir.ActivationFunctionType
+ALU = mybir.AluOpType
+AXIS = mybir.AxisListType
+
+P = 128
+PACK = 4
+K_PASS = P * PACK
+
+C = 16384
+T = 2
+V = 128
+IC = 512
+COLS = T * V
+PASSES = C // K_PASS
+CHUNK = 4
+CHUNKS = PASSES // CHUNK
+O_TILES = IC // P
+HALVES = (IC * T) // K_PASS
+RUN = 4
+
+FLOPS = 2 * 2 * IC * C * COLS + 2 * V * V * IC * T
+
+
+def load_scale_planes(queue, view, planes, scales):
+    by_block = scales.rearrange("(c i) q n -> q i c n", i=CHUNK)
+    for quadrant in range(4):
+        for r in range(4):
+            first = 32 * quadrant + r
+            queue.dma_start(
+                out=planes[first : first + 4 * CHUNK : 4, :, :].bitcast(view),
+                in_=by_block[4 * quadrant + r].bitcast(view),
+            )
+
+
+def regroup(copy, grouped, raw):
+    copy(
+        out=grouped.rearrange("p (c i j) -> p c j i", i=RUN, j=PACK),
+        in_=raw.rearrange("p (j c i) -> p c j i", j=PACK, i=RUN),
+    )
+
+
+def project(nc, acc, w_words, w_planes, x_codes, x_planes, c):
+    for m in range(O_TILES):
+        o_cols = slice(m * P, (m + 1) * P)
+        for i in range(CHUNK):
+            g = c * CHUNK + i
+            nc.tensor.matmul_mx(
+                out=acc[m][:],
+                lhsT=w_words[:, i, o_cols].bitcast(FP8X4),
+                lhsT_scale=w_planes[4 * i : P, c, o_cols],
+                rhs=x_codes[:, g, :].bitcast(FP8X4),
+                rhs_scale=x_planes[:, g, :],
+                start=(g == 0),
+                stop=(g == PASSES - 1),
+            )
+
+
+def leave_psum_and_quantise(nc, acc, bias, grouped, codes, planes):
+    for m in range(O_TILES):
+        h, u = divmod(m, 2)
+        dst = grouped[:, h, :, 2 * u : 2 * u + 2]
+        src = acc[m][:].rearrange("p (t v) -> p v t", t=T)
+        if h == 0:
+            nc.scalar.activation(out=dst, in_=src, func=ACT.Identity, bias=bias[:, m : m + 1])
+        else:
+            nc.vector.tensor_scalar_add(out=dst, in0=src, scalar1=bias[:, m : m + 1])
+    nc.vector.quantize_mx(
+        out=codes[:].rearrange("p h v -> p (h v)").bitcast(FP8X4),
+        scales=planes[:].rearrange("p h v -> p (h v)"),
+        in_=grouped[:].rearrange("p h v j -> p (h v j)"),
+    )
+
+
+def tile_adaptivegraphconstruction_k_kernel(
+    tc, x, Wa_words, Wa_scales, ba, Wb_words, Wb_scales, bb, A, alpha, out
+):
+    nc = tc.nc
+    x_chunks = x[0].rearrange("(c i p j) t v -> c p i (j t v)", i=CHUNK, p=P, j=PACK)
+    wa_chunks = Wa_words.rearrange("(c i) p n t -> c p i (n t)", i=CHUNK)
+    wb_chunks = Wb_words.rearrange("(c i) p n t -> c p i (n t)", i=CHUNK)
+
+    with ExitStack() as stack:
+        stack.enter_context(tc.manual_schedule())
+        keep = stack.enter_context(tc.tile_pool(name="keep", bufs=1))
+        x_stage = stack.enter_context(tc.tile_pool(name="x_stage", bufs=3))
+        w_stage = stack.enter_context(tc.tile_pool(name="w_stage", bufs=6))
+        banks = stack.enter_context(tc.psum_pool(name="banks", bufs=1))
+
+        x_codes = keep.tile([P, PASSES, COLS], U32, align_bytes=64)
+        x_planes = keep.tile([P, PASSES, COLS], U8, align_bytes=64)
+        wa_planes = keep.tile([P, CHUNKS, IC], U8, align_bytes=64)
+        wb_planes = keep.tile([P, CHUNKS, IC], U8, align_bytes=64)
+
+        def fetch_x(c):
+            raw = x_stage.tile([P, CHUNK, PACK * COLS], BF16)
+            nc.sync.dma_start(out=raw[:], in_=x_chunks[c])
+            return raw
+
+        def fetch_w(chunks, c):
+            w_words = w_stage.tile([P, CHUNK, IC], U32, align_bytes=64)
+            nc.sync.dma_start(out=w_words[:].bitcast(I32), in_=chunks[c].bitcast(I32))
+            return w_words
+
+        def regroup_x(raw):
+            grouped = x_stage.tile([P, CHUNK, COLS * PACK], BF16, align_bytes=64)
+            for i in range(CHUNK):
+                copy = nc.vector.tensor_copy if i % 2 == 0 else nc.scalar.copy
+                regroup(copy, grouped[:, i, :], raw[:, i, :])
+            return grouped
+
+        nc.vector.memset(wa_planes[:].bitcast(I32), 0)
+        nc.vector.memset(wb_planes[:].bitcast(I32), 0)
+        raw = fetch_x(0)
+        load_scale_planes(nc.sync, I32, wa_planes, Wa_scales)
+
+        load_scale_planes(nc.gpsimd, F32, wb_planes, Wb_scales)
+        ident = keep.tile([P, P], BF16)
+        make_identity(nc, ident[:])
+
+        zero = keep.tile([P, 1], F32)
+        nc.vector.memset(zero[:], 0.0)
+        warm = keep.tile([P, 1], F32)
+        nc.scalar.activation(out=warm[:], in_=zero[:], func=ACT.Tanh)
+        bias_rows = keep.tile([P, P], BF16)
+        nc.vector.memset(bias_rows[:], 0.0)
+
+        grouped = regroup_x(raw)
+
+        nc.scalar.dma_start(out=bias_rows[0:O_TILES, :], in_=ba.rearrange("(m p) -> m p", p=P))
+        nc.scalar.dma_start(
+            out=bias_rows[O_TILES : 2 * O_TILES, :], in_=bb.rearrange("(m p) -> m p", p=P)
+        )
+        a_sb = keep.tile([P, V], BF16)
+        nc.scalar.dma_start(out=a_sb[:], in_=A[0])
+        alpha_bf = keep.tile([P, 1], BF16)
+        nc.scalar.dma_start(out=alpha_bf[:], in_=alpha.partition_broadcast(P))
+
+        bias_ps = banks.tile([P, P], BF16, tag="bank7")
+        nc.tensor.transpose(bias_ps[:], bias_rows[:], ident[:])
+
+        qa_acc = [banks.tile([P, COLS], F32, name="qa_acc%d" % m, tag="bank%d" % m) for m in range(O_TILES)]
+        for c in range(CHUNKS):
+            this_grouped = grouped
+            if c + 1 < CHUNKS:
+                raw = fetch_x(c + 1)
+            wa_words = fetch_w(wa_chunks, c)
+            if c + 1 < CHUNKS:
+                grouped = regroup_x(raw)
+            passes = slice(c * CHUNK, (c + 1) * CHUNK)
+            nc.vector.quantize_mx(
+                out=x_codes[:, passes, :].rearrange("p g w -> p (g w)").bitcast(FP8X4),
+                scales=x_planes[:, passes, :].rearrange("p g w -> p (g w)"),
+                in_=this_grouped[:].rearrange("p g w -> p (g w)"),
+            )
+            project(nc, qa_acc, wa_words, wa_planes, x_codes, x_planes, c)
+
+        bias = keep.tile([P, 2 * O_TILES], F32)
+        nc.vector.tensor_copy(out=bias[:], in_=bias_ps[:, 0 : 2 * O_TILES])
+        alpha_sb = keep.tile([P, 1], F32)
+        nc.vector.tensor_copy(out=alpha_sb[:], in_=alpha_bf[:])
+
+        q_grouped = keep.tile([P, HALVES, V, PACK], BF16, align_bytes=64)
+        q_codes = keep.tile([P, HALVES, V], U32, align_bytes=64)
+        q_planes = keep.tile([P, HALVES, V], U8, align_bytes=64)
+        leave_psum_and_quantise(nc, qa_acc, bias[:, 0:O_TILES], q_grouped, q_codes, q_planes)
+
+        kb_acc = [
+            banks.tile([P, COLS], F32, name="kb_acc%d" % m, tag="bank%d" % (O_TILES + m))
+            for m in range(O_TILES)
+        ]
+        for c in range(CHUNKS):
+            wb_words = fetch_w(wb_chunks, c)
+            project(nc, kb_acc, wb_words, wb_planes, x_codes, x_planes, c)
+
+        k_grouped = keep.tile([P, HALVES, V, PACK], BF16, align_bytes=64)
+        k_codes = keep.tile([P, HALVES, V], U32, align_bytes=64)
+        k_planes = keep.tile([P, HALVES, V], U8, align_bytes=64)
+        leave_psum_and_quantise(
+            nc, kb_acc, bias[:, O_TILES : 2 * O_TILES], k_grouped, k_codes, k_planes
+        )
+
+        g_ps = banks.tile([P, V], F32, tag="bank0")
+        for h in range(HALVES):
+            nc.tensor.matmul_mx(
+                out=g_ps[:],
+                lhsT=q_codes[:, h, :].bitcast(FP8X4),
+                lhsT_scale=q_planes[:, h, :],
+                rhs=k_codes[:, h, :].bitcast(FP8X4),
+                rhs_scale=k_planes[:, h, :],
+                start=(h == 0),
+                stop=(h == HALVES - 1),
+            )
+        graph_b = keep.tile([P, V], F32)
+        nc.scalar.activation(out=graph_b[:], in_=g_ps[:], func=ACT.Tanh, scale=1.0 / (IC * T))
+        z = keep.tile([P, V], F32)
+        nc.vector.scalar_tensor_tensor(
+            out=z[:], in0=graph_b[:], scalar=alpha_sb[:, 0:1], in1=a_sb[:], op0=ALU.mult, op1=ALU.add
+        )
+        neg_max = keep.tile([P, 1], F32)
+        nc.vector.tensor_reduce(out=neg_max[:], in_=z[:], axis=AXIS.X, op=ALU.max, negate=True)
+        e = keep.tile([P, V], F32)
+        e_sum = keep.tile([P, 1], F32)
+        nc.scalar.activation(
+            out=e[:], in_=z[:], func=ACT.Exp, bias=neg_max[:, 0:1], accum_out=e_sum[:]
+        )
+        inv_sum = keep.tile([P, 1], F32)
+        nc.vector.reciprocal(out=inv_sum[:], in_=e_sum[:])
+        prob = keep.tile([P, V], F32)
+        nc.vector.tensor_scalar_mul(out=prob[:], in0=e[:], scalar1=inv_sum[:, 0:1])
+        nc.sync.dma_start(out=out[0], in_=prob[:])

@@ -124,9 +124,9 @@ def tile_adaptivegraphconstruction_k_kernel(
         raw = fetch_x(0)
         load_scale_planes(nc.sync, I32, wa_planes, Wa_scales)
 
-        load_scale_planes(nc.gpsimd, F32, wb_planes, Wb_scales)
         ident = keep.tile([P, P], BF16)
         make_identity(nc, ident[:])
+        load_scale_planes(nc.gpsimd, F32, wb_planes, Wb_scales)
 
         zero = keep.tile([P, 1], F32)
         nc.vector.memset(zero[:], 0.0)

@@ -94,7 +94,7 @@ def tile_adaptivegraphconstruction_k_kernel(
         stack.enter_context(tc.manual_schedule())
         keep = stack.enter_context(tc.tile_pool(name="keep", bufs=1))
         x_stage = stack.enter_context(tc.tile_pool(name="x_stage", bufs=3))
-        w_stage = stack.enter_context(tc.tile_pool(name="w_stage", bufs=6))
+        w_stage = stack.enter_context(tc.tile_pool(name="w_stage", bufs=8))
         banks = stack.enter_context(tc.psum_pool(name="banks", bufs=1))
 
         x_codes = keep.tile([P, PASSES, COLS], U32, align_bytes=64)
@@ -122,10 +122,10 @@ def tile_adaptivegraphconstruction_k_kernel(
         nc.vector.memset(wa_planes[:].bitcast(I32), 0)
         nc.vector.memset(wb_planes[:].bitcast(I32), 0)
         raw = fetch_x(0)
-        load_scale_planes(nc.sync, I32, wa_planes, Wa_scales)
 
         ident = keep.tile([P, P], BF16)
         make_identity(nc, ident[:])
+        load_scale_planes(nc.gpsimd, F32, wa_planes, Wa_scales)
         load_scale_planes(nc.gpsimd, F32, wb_planes, Wb_scales)
 
         zero = keep.tile([P, 1], F32)

@@ -134,6 +134,10 @@ def tile_adaptivegraphconstruction_k_kernel(
         nc.scalar.activation(out=warm[:], in_=zero[:], func=ACT.Tanh)
         bias_rows = keep.tile([P, P], BF16)
         nc.vector.memset(bias_rows[:], 0.0)
+        ones = keep.tile([P, P], BF16)
+        nc.vector.memset(ones[:], 1.0)
+        alpha_row = keep.tile([P, 2], BF16)
+        nc.vector.memset(alpha_row[:], 0.0)
 
         grouped = regroup_x(raw)
 
@@ -143,11 +147,7 @@ def tile_adaptivegraphconstruction_k_kernel(
         )
         a_sb = keep.tile([P, V], BF16)
         nc.scalar.dma_start(out=a_sb[:], in_=A[0])
-        alpha_bf = keep.tile([P, 1], BF16)
-        nc.scalar.dma_start(out=alpha_bf[:], in_=alpha.partition_broadcast(P))
-
-        bias_ps = banks.tile([P, P], BF16, tag="bank7")
-        nc.tensor.transpose(bias_ps[:], bias_rows[:], ident[:])
+        nc.scalar.dma_start(out=alpha_row[0:1, 0:1], in_=alpha.unsqueeze(0))
 
         qa_acc = [banks.tile([P, COLS], F32, name="qa_acc%d" % m, tag="bank%d" % m) for m in range(O_TILES)]
         for c in range(CHUNKS):
@@ -165,10 +165,14 @@ def tile_adaptivegraphconstruction_k_kernel(
             )
             project(nc, qa_acc, wa_words, wa_planes, x_codes, x_planes, c)
 
+        bias_ps = banks.tile([P, P], BF16, tag="bank7")
+        nc.tensor.transpose(bias_ps[:], bias_rows[:], ident[:])
+        alpha_ps = banks.tile([P, 2], F32, tag="bank6")
+        nc.tensor.matmul(alpha_ps[:], lhsT=ones[:], rhs=alpha_row[:], start=True, stop=True)
         bias = keep.tile([P, 2 * O_TILES], F32)
         nc.vector.tensor_copy(out=bias[:], in_=bias_ps[:, 0 : 2 * O_TILES])
         alpha_sb = keep.tile([P, 1], F32)
-        nc.vector.tensor_copy(out=alpha_sb[:], in_=alpha_bf[:])
+        nc.vector.tensor_copy(out=alpha_sb[:], in_=alpha_ps[:, 0:1])
 
         q_grouped = keep.tile([P, HALVES, V, PACK], BF16, align_bytes=64)
         q_codes = keep.tile([P, HALVES, V], U32, align_bytes=64)

@@ -50,15 +50,15 @@ def regroup(copy, grouped, raw):
     )
 
 
-def project(nc, acc, w_words, w_planes, x_codes, x_planes, c):
-    for m in range(O_TILES):
+def project(nc, acc, w_words, w_planes, x_codes, x_planes, first):
+    for m in (0, 2, 1, 3):
         o_cols = slice(m * P, (m + 1) * P)
-        for i in range(CHUNK):
-            g = c * CHUNK + i
+        for i in range(w_words.shape[1]):
+            g = first + i
             nc.tensor.matmul_mx(
                 out=acc[m][:],
                 lhsT=w_words[:, i, o_cols].bitcast(FP8X4),
-                lhsT_scale=w_planes[4 * i : P, c, o_cols],
+                lhsT_scale=w_planes[4 * (g % CHUNK) : P, g // CHUNK, o_cols],
                 rhs=x_codes[:, g, :].bitcast(FP8X4),
                 rhs_scale=x_planes[:, g, :],
                 start=(g == 0),
@@ -75,11 +75,12 @@ def leave_psum_and_quantise(nc, acc, bias, grouped, codes, planes):
             nc.scalar.activation(out=dst, in_=src, func=ACT.Identity, bias=bias[:, m : m + 1])
         else:
             nc.vector.tensor_scalar_add(out=dst, in0=src, scalar1=bias[:, m : m + 1])
-    nc.vector.quantize_mx(
-        out=codes[:].rearrange("p h v -> p (h v)").bitcast(FP8X4),
-        scales=planes[:].rearrange("p h v -> p (h v)"),
-        in_=grouped[:].rearrange("p h v j -> p (h v j)"),
-    )
+    for h in range(HALVES):
+        nc.vector.quantize_mx(
+            out=codes[:, h, :].bitcast(FP8X4),
+            scales=planes[:, h, :],
+            in_=grouped[:, h, :, :].rearrange("p v j -> p (v j)"),
+        )
 
 
 def tile_adaptivegraphconstruction_k_kernel(
@@ -87,8 +88,8 @@ def tile_adaptivegraphconstruction_k_kernel(
 ):
     nc = tc.nc
     x_chunks = x[0].rearrange("(c i p j) t v -> c p i (j t v)", i=CHUNK, p=P, j=PACK)
-    wa_chunks = Wa_words.rearrange("(c i) p n t -> c p i (n t)", i=CHUNK)
-    wb_chunks = Wb_words.rearrange("(c i) p n t -> c p i (n t)", i=CHUNK)
+    wa_passes = Wa_words.rearrange("g p n t -> p g (n t)")
+    wb_passes = Wb_words.rearrange("g p n t -> p g (n t)")
 
     with ExitStack() as stack:
         stack.enter_context(tc.manual_schedule())
@@ -107,9 +108,11 @@ def tile_adaptivegraphconstruction_k_kernel(
             nc.sync.dma_start(out=raw[:], in_=x_chunks[c])
             return raw
 
-        def fetch_w(chunks, c):
-            w_words = w_stage.tile([P, CHUNK, IC], U32, align_bytes=64)
-            nc.sync.dma_start(out=w_words[:].bitcast(I32), in_=chunks[c].bitcast(I32))
+        def fetch_w(passes_in_hbm, first, count):
+            w_words = w_stage.tile([P, count, IC], U32, align_bytes=64)
+            nc.sync.dma_start(
+                out=w_words[:].bitcast(I32), in_=passes_in_hbm[:, first : first + count, :].bitcast(I32)
+            )
             return w_words
 
         def regroup_x(raw):
@@ -154,7 +157,7 @@ def tile_adaptivegraphconstruction_k_kernel(
             this_grouped = grouped
             if c + 1 < CHUNKS:
                 raw = fetch_x(c + 1)
-            wa_words = fetch_w(wa_chunks, c)
+            wa_words = fetch_w(wa_passes, c * CHUNK, CHUNK)
             if c + 1 < CHUNKS:
                 grouped = regroup_x(raw)
             passes = slice(c * CHUNK, (c + 1) * CHUNK)
@@ -163,7 +166,7 @@ def tile_adaptivegraphconstruction_k_kernel(
                 scales=x_planes[:, passes, :].rearrange("p g w -> p (g w)"),
                 in_=this_grouped[:].rearrange("p g w -> p (g w)"),
             )
-            project(nc, qa_acc, wa_words, wa_planes, x_codes, x_planes, c)
+            project(nc, qa_acc, wa_words, wa_planes, x_codes, x_planes, c * CHUNK)
 
         bias_ps = banks.tile([P, P], BF16, tag="bank7")
         nc.tensor.transpose(bias_ps[:], bias_rows[:], ident[:])
@@ -183,9 +186,11 @@ def tile_adaptivegraphconstruction_k_kernel(
             banks.tile([P, COLS], F32, name="kb_acc%d" % m, tag="bank%d" % (O_TILES + m))
             for m in range(O_TILES)
         ]
-        for c in range(CHUNKS):
-            wb_words = fetch_w(wb_chunks, c)
-            project(nc, kb_acc, wb_words, wb_planes, x_codes, x_planes, c)
+        first = 0
+        for count in [CHUNK] * (CHUNKS - 1) + [2, 1, 1]:
+            wb_words = fetch_w(wb_passes, first, count)
+            project(nc, kb_acc, wb_words, wb_planes, x_codes, x_planes, first)
+            first += count
 
         k_grouped = keep.tile([P, HALVES, V, PACK], BF16, align_bytes=64)
         k_codes = keep.tile([P, HALVES, V], U32, align_bytes=64)

@@ -32,15 +32,14 @@ RUN = 4
 FLOPS = 2 * 2 * IC * C * COLS + 2 * V * V * IC * T
 
 
-def load_scale_planes(queue, view, planes, scales):
+def load_scale_rows(nc, planes, scales, r):
     by_block = scales.rearrange("(c i) q n -> q i c n", i=CHUNK)
     for quadrant in range(4):
-        for r in range(4):
-            first = 32 * quadrant + r
-            queue.dma_start(
-                out=planes[first : first + 4 * CHUNK : 4, :, :].bitcast(view),
-                in_=by_block[4 * quadrant + r].bitcast(view),
-            )
+        first = 32 * quadrant + r
+        nc.sync.dma_start(
+            out=planes[first : first + 4 * CHUNK : 4, :, :].bitcast(I32),
+            in_=by_block[4 * quadrant + r].bitcast(I32),
+        )
 
 
 def regroup(copy, grouped, raw):
@@ -124,13 +123,13 @@ def tile_adaptivegraphconstruction_k_kernel(
 
         nc.vector.memset(wa_planes[:].bitcast(I32), 0)
         nc.vector.memset(wb_planes[:].bitcast(I32), 0)
-        raw = fetch_x(0)
+        raws = []
+        for c in range(2):
+            raws.append(fetch_x(c))
+            load_scale_rows(nc, wa_planes, Wa_scales, c)
 
         ident = keep.tile([P, P], BF16)
         make_identity(nc, ident[:])
-        load_scale_planes(nc.gpsimd, F32, wa_planes, Wa_scales)
-        load_scale_planes(nc.gpsimd, F32, wb_planes, Wb_scales)
-
         zero = keep.tile([P, 1], F32)
         nc.vector.memset(zero[:], 0.0)
         warm = keep.tile([P, 1], F32)
@@ -142,7 +141,7 @@ def tile_adaptivegraphconstruction_k_kernel(
         alpha_row = keep.tile([P, 2], BF16)
         nc.vector.memset(alpha_row[:], 0.0)
 
-        grouped = regroup_x(raw)
+        grouped = regroup_x(raws[0])
 
         nc.scalar.dma_start(out=bias_rows[0:O_TILES, :], in_=ba.rearrange("(m p) -> m p", p=P))
         nc.scalar.dma_start(
@@ -155,11 +154,17 @@ def tile_adaptivegraphconstruction_k_kernel(
         qa_acc = [banks.tile([P, COLS], F32, name="qa_acc%d" % m, tag="bank%d" % m) for m in range(O_TILES)]
         for c in range(CHUNKS):
             this_grouped = grouped
-            if c + 1 < CHUNKS:
-                raw = fetch_x(c + 1)
             wa_words = fetch_w(wa_passes, c * CHUNK, CHUNK)
+            if c == 0:
+                load_scale_rows(nc, wa_planes, Wa_scales, 2)
+            if c >= 4:
+                load_scale_rows(nc, wb_planes, Wb_scales, c - 4)
+            if c + 2 < CHUNKS:
+                raws.append(fetch_x(c + 2))
+            if c == 0:
+                load_scale_rows(nc, wa_planes, Wa_scales, 3)
             if c + 1 < CHUNKS:
-                grouped = regroup_x(raw)
+                grouped = regroup_x(raws[c + 1])
             passes = slice(c * CHUNK, (c + 1) * CHUNK)
             nc.vector.quantize_mx(
                 out=x_codes[:, passes, :].rearrange("p g w -> p (g w)").bitcast(FP8X4),

@@ -32,13 +32,13 @@ RUN = 4
 FLOPS = 2 * 2 * IC * C * COLS + 2 * V * V * IC * T
 
 
-def load_scale_rows(nc, planes, scales, r):
+def load_scale_rows(queue, view, planes, scales, r):
     by_block = scales.rearrange("(c i) q n -> q i c n", i=CHUNK)
     for quadrant in range(4):
         first = 32 * quadrant + r
-        nc.sync.dma_start(
-            out=planes[first : first + 4 * CHUNK : 4, :, :].bitcast(I32),
-            in_=by_block[4 * quadrant + r].bitcast(I32),
+        queue.dma_start(
+            out=planes[first : first + 4 * CHUNK : 4, :, :].bitcast(view),
+            in_=by_block[4 * quadrant + r].bitcast(view),
         )
 
 
@@ -126,8 +126,10 @@ def tile_adaptivegraphconstruction_k_kernel(
         raws = []
         for c in range(2):
             raws.append(fetch_x(c))
-            load_scale_rows(nc, wa_planes, Wa_scales, c)
+            load_scale_rows(nc.sync, I32, wa_planes, Wa_scales, c)
 
+        for r in range(4):
+            load_scale_rows(nc.gpsimd, F32, wb_planes, Wb_scales, r)
         ident = keep.tile([P, P], BF16)
         make_identity(nc, ident[:])
         zero = keep.tile([P, 1], F32)
@@ -156,13 +158,11 @@ def tile_adaptivegraphconstruction_k_kernel(
             this_grouped = grouped
             wa_words = fetch_w(wa_passes, c * CHUNK, CHUNK)
             if c == 0:
-                load_scale_rows(nc, wa_planes, Wa_scales, 2)
-            if c >= 4:
-                load_scale_rows(nc, wb_planes, Wb_scales, c - 4)
+                load_scale_rows(nc.sync, I32, wa_planes, Wa_scales, 2)
             if c + 2 < CHUNKS:
                 raws.append(fetch_x(c + 2))
             if c == 0:
-                load_scale_rows(nc, wa_planes, Wa_scales, 3)
+                load_scale_rows(nc.sync, I32, wa_planes, Wa_scales, 3)
             if c + 1 < CHUNKS:
                 grouped = regroup_x(raws[c + 1])
             passes = slice(c * CHUNK, (c + 1) * CHUNK)

@@ -86,9 +86,9 @@ def tile_adaptivegraphconstruction_k_kernel(
     tc, x, Wa_words, Wa_scales, ba, Wb_words, Wb_scales, bb, A, alpha, out
 ):
     nc = tc.nc
-    x_chunks = x[0].rearrange("(c i p j) t v -> c p i (j t v)", i=CHUNK, p=P, j=PACK)
-    wa_passes = Wa_words.rearrange("g p n t -> p g (n t)")
-    wb_passes = Wb_words.rearrange("g p n t -> p g (n t)")
+    x_passes = x[0].rearrange("(g p j) t v -> g p (j t v)", p=P, j=PACK)
+    wa_passes = Wa_words.rearrange("g p n t -> g p (n t)")
+    wb_passes = Wb_words.rearrange("g p n t -> g p (n t)")
 
     with ExitStack() as stack:
         stack.enter_context(tc.manual_schedule())
@@ -104,14 +104,16 @@ def tile_adaptivegraphconstruction_k_kernel(
 
         def fetch_x(c):
             raw = x_stage.tile([P, CHUNK, PACK * COLS], BF16)
-            nc.sync.dma_start(out=raw[:], in_=x_chunks[c])
+            for i in range(CHUNK):
+                nc.sync.dma_start(out=raw[:, i, :], in_=x_passes[c * CHUNK + i])
             return raw
 
         def fetch_w(passes_in_hbm, first, count):
             w_words = w_stage.tile([P, count, IC], U32, align_bytes=64)
-            nc.sync.dma_start(
-                out=w_words[:].bitcast(I32), in_=passes_in_hbm[:, first : first + count, :].bitcast(I32)
-            )
+            for i in range(count):
+                nc.sync.dma_start(
+                    out=w_words[:, i, :].bitcast(I32), in_=passes_in_hbm[first + i].bitcast(I32)
+                )
             return w_words
 
         def regroup_x(raw):
@@ -192,7 +194,7 @@ def tile_adaptivegraphconstruction_k_kernel(
             for m in range(O_TILES)
         ]
         first = 0
-        for count in [CHUNK] * (CHUNKS - 1) + [2, 1, 1]:
+        for count in [CHUNK] * (CHUNKS - 1) + [1] * CHUNK:
             wb_words = fetch_w(wb_passes, first, count)
             project(nc, kb_acc, wb_words, wb_planes, x_codes, x_planes, first)
             first += count

@@ -32,14 +32,29 @@ RUN = 4
 FLOPS = 2 * 2 * IC * C * COLS + 2 * V * V * IC * T
 
 
-def load_scale_rows(queue, view, planes, scales, r):
+X_LEAD = 2
+WB_LAG = 4
+WA_EARLY = 6
+WB_EARLY = 2
+
+
+def load_scales_of_chunk(nc, planes, scales, c):
+    for quadrant in range(4):
+        nc.sync.dma_start(
+            out=planes[32 * quadrant : 32 * quadrant + 4 * CHUNK, c, :].bitcast(I32),
+            in_=scales[CHUNK * c : CHUNK * (c + 1), 4 * quadrant : 4 * quadrant + 4, :].bitcast(I32),
+        )
+
+
+def load_later_scales(nc, planes, scales, c0):
     by_block = scales.rearrange("(c i) q n -> q i c n", i=CHUNK)
     for quadrant in range(4):
-        first = 32 * quadrant + r
-        queue.dma_start(
-            out=planes[first : first + 4 * CHUNK : 4, :, :].bitcast(view),
-            in_=by_block[4 * quadrant + r].bitcast(view),
-        )
+        for r in range(4):
+            first = 32 * quadrant + r
+            nc.gpsimd.dma_start(
+                out=planes[first : first + 4 * CHUNK : 4, c0:, :].bitcast(F32),
+                in_=by_block[4 * quadrant + r][:, c0:, :].bitcast(F32),
+            )
 
 
 def regroup(copy, grouped, raw):
@@ -49,20 +64,18 @@ def regroup(copy, grouped, raw):
     )
 
 
-def project(nc, acc, w_words, w_planes, x_codes, x_planes, first):
+def project(nc, acc, w_words, w_planes, x_codes, x_planes, g):
     for m in (0, 2, 1, 3):
         o_cols = slice(m * P, (m + 1) * P)
-        for i in range(w_words.shape[1]):
-            g = first + i
-            nc.tensor.matmul_mx(
-                out=acc[m][:],
-                lhsT=w_words[:, i, o_cols].bitcast(FP8X4),
-                lhsT_scale=w_planes[4 * (g % CHUNK) : P, g // CHUNK, o_cols],
-                rhs=x_codes[:, g, :].bitcast(FP8X4),
-                rhs_scale=x_planes[:, g, :],
-                start=(g == 0),
-                stop=(g == PASSES - 1),
-            )
+        nc.tensor.matmul_mx(
+            out=acc[m][:],
+            lhsT=w_words[:, o_cols].bitcast(FP8X4),
+            lhsT_scale=w_planes[4 * (g % CHUNK) : P, g // CHUNK, o_cols],
+            rhs=x_codes[:, g, :].bitcast(FP8X4),
+            rhs_scale=x_planes[:, g, :],
+            start=(g == 0),
+            stop=(g == PASSES - 1),
+        )
 
 
 def leave_psum_and_quantise(nc, acc, bias, grouped, codes, planes):
@@ -93,8 +106,8 @@ def tile_adaptivegraphconstruction_k_kernel(
     with ExitStack() as stack:
         stack.enter_context(tc.manual_schedule())
         keep = stack.enter_context(tc.tile_pool(name="keep", bufs=1))
-        x_stage = stack.enter_context(tc.tile_pool(name="x_stage", bufs=3))
-        w_stage = stack.enter_context(tc.tile_pool(name="w_stage", bufs=8))
+        x_stage = stack.enter_context(tc.tile_pool(name="x_stage", bufs=6))
+        w_stage = stack.enter_context(tc.tile_pool(name="w_stage", bufs=20))
         banks = stack.enter_context(tc.psum_pool(name="banks", bufs=1))
 
         x_codes = keep.tile([P, PASSES, COLS], U32, align_bytes=64)
@@ -102,78 +115,59 @@ def tile_adaptivegraphconstruction_k_kernel(
         wa_planes = keep.tile([P, CHUNKS, IC], U8, align_bytes=64)
         wb_planes = keep.tile([P, CHUNKS, IC], U8, align_bytes=64)
 
-        def fetch_x(c):
-            raw = x_stage.tile([P, CHUNK, PACK * COLS], BF16)
-            for i in range(CHUNK):
-                nc.sync.dma_start(out=raw[:, i, :], in_=x_passes[c * CHUNK + i])
+        def fetch_x(g):
+            raw = x_stage.tile([P, PACK * COLS], BF16)
+            nc.sync.dma_start(out=raw[:], in_=x_passes[g])
             return raw
 
-        def fetch_w(passes_in_hbm, first, count):
-            w_words = w_stage.tile([P, count, IC], U32, align_bytes=64)
-            for i in range(count):
-                nc.sync.dma_start(
-                    out=w_words[:, i, :].bitcast(I32), in_=passes_in_hbm[first + i].bitcast(I32)
-                )
-            return w_words
+        def quantise_x(g, raw):
+            grouped = x_stage.tile([P, COLS * PACK], BF16, align_bytes=64)
+            regroup(nc.scalar.copy, grouped[:], raw[:])
+            nc.vector.quantize_mx(
+                out=x_codes[:, g, :].bitcast(FP8X4), scales=x_planes[:, g, :], in_=grouped[:]
+            )
 
-        def regroup_x(raw):
-            grouped = x_stage.tile([P, CHUNK, COLS * PACK], BF16, align_bytes=64)
-            for i in range(CHUNK):
-                copy = nc.vector.tensor_copy if i % 2 == 0 else nc.scalar.copy
-                regroup(copy, grouped[:, i, :], raw[:, i, :])
-            return grouped
+        def fetch_wa(g):
+            wa_words = w_stage.tile([P, IC], U32, align_bytes=64)
+            nc.sync.dma_start(out=wa_words[:].bitcast(I32), in_=wa_passes[g].bitcast(I32))
+            return wa_words
 
-        nc.vector.memset(wa_planes[:].bitcast(I32), 0)
-        nc.vector.memset(wb_planes[:].bitcast(I32), 0)
-        raws = []
-        for c in range(2):
-            raws.append(fetch_x(c))
-            load_scale_rows(nc.sync, I32, wa_planes, Wa_scales, c)
+        def fetch_wb(g):
+            wb_words = w_stage.tile([P, IC], U32, align_bytes=64)
+            nc.sync.dma_start(out=wb_words[:].bitcast(I32), in_=wb_passes[g].bitcast(I32))
+            return wb_words
 
-        for r in range(4):
-            load_scale_rows(nc.gpsimd, F32, wb_planes, Wb_scales, r)
-        ident = keep.tile([P, P], BF16)
-        make_identity(nc, ident[:])
-        zero = keep.tile([P, 1], F32)
-        nc.vector.memset(zero[:], 0.0)
-        warm = keep.tile([P, 1], F32)
-        nc.scalar.activation(out=warm[:], in_=zero[:], func=ACT.Tanh)
         bias_rows = keep.tile([P, P], BF16)
         nc.vector.memset(bias_rows[:], 0.0)
-        ones = keep.tile([P, P], BF16)
-        nc.vector.memset(ones[:], 1.0)
         alpha_row = keep.tile([P, 2], BF16)
         nc.vector.memset(alpha_row[:], 0.0)
-
-        grouped = regroup_x(raws[0])
+        nc.vector.memset(wa_planes[:, 0:1, :].bitcast(I32), 0)
+        nc.vector.memset(wb_planes[:].bitcast(I32), 0)
+        nc.vector.memset(wa_planes[:, 1:CHUNKS, :].bitcast(I32), 0)
+        ones = keep.tile([P, P], BF16)
+        nc.vector.memset(ones[:], 1.0)
+        zero = keep.tile([P, 1], F32)
+        nc.vector.memset(zero[:], 0.0)
 
         nc.scalar.dma_start(out=bias_rows[0:O_TILES, :], in_=ba.rearrange("(m p) -> m p", p=P))
         nc.scalar.dma_start(
             out=bias_rows[O_TILES : 2 * O_TILES, :], in_=bb.rearrange("(m p) -> m p", p=P)
         )
+        nc.scalar.dma_start(out=alpha_row[0:1, 0:1], in_=alpha.unsqueeze(0))
         a_sb = keep.tile([P, V], BF16)
         nc.scalar.dma_start(out=a_sb[:], in_=A[0])
-        nc.scalar.dma_start(out=alpha_row[0:1, 0:1], in_=alpha.unsqueeze(0))
+        warm = keep.tile([P, 1], F32)
+        nc.scalar.activation(out=warm[:], in_=zero[:], func=ACT.Tanh)
 
-        qa_acc = [banks.tile([P, COLS], F32, name="qa_acc%d" % m, tag="bank%d" % m) for m in range(O_TILES)]
-        for c in range(CHUNKS):
-            this_grouped = grouped
-            wa_words = fetch_w(wa_passes, c * CHUNK, CHUNK)
-            if c == 0:
-                load_scale_rows(nc.sync, I32, wa_planes, Wa_scales, 2)
-            if c + 2 < CHUNKS:
-                raws.append(fetch_x(c + 2))
-            if c == 0:
-                load_scale_rows(nc.sync, I32, wa_planes, Wa_scales, 3)
-            if c + 1 < CHUNKS:
-                grouped = regroup_x(raws[c + 1])
-            passes = slice(c * CHUNK, (c + 1) * CHUNK)
-            nc.vector.quantize_mx(
-                out=x_codes[:, passes, :].rearrange("p g w -> p (g w)").bitcast(FP8X4),
-                scales=x_planes[:, passes, :].rearrange("p g w -> p (g w)"),
-                in_=this_grouped[:].rearrange("p g w -> p (g w)"),
-            )
-            project(nc, qa_acc, wa_words, wa_planes, x_codes, x_planes, c * CHUNK)
+        ident = keep.tile([P, P], BF16)
+        make_identity(nc, ident[:])
+        load_later_scales(nc, wb_planes, Wb_scales, WB_EARLY)
+        load_later_scales(nc, wa_planes, Wa_scales, WA_EARLY)
+
+        for g in range(X_LEAD):
+            quantise_x(g, fetch_x(g))
+            if g == 0:
+                load_scales_of_chunk(nc, wa_planes, Wa_scales, 0)
 
         bias_ps = banks.tile([P, P], BF16, tag="bank7")
         nc.tensor.transpose(bias_ps[:], bias_rows[:], ident[:])
@@ -184,20 +178,32 @@ def tile_adaptivegraphconstruction_k_kernel(
         alpha_sb = keep.tile([P, 1], F32)
         nc.vector.tensor_copy(out=alpha_sb[:], in_=alpha_ps[:, 0:1])
 
-        q_grouped = keep.tile([P, HALVES, V, PACK], BF16, align_bytes=64)
-        q_codes = keep.tile([P, HALVES, V], U32, align_bytes=64)
-        q_planes = keep.tile([P, HALVES, V], U8, align_bytes=64)
-        leave_psum_and_quantise(nc, qa_acc, bias[:, 0:O_TILES], q_grouped, q_codes, q_planes)
-
+        qa_acc = [banks.tile([P, COLS], F32, name="qa_acc%d" % m, tag="bank%d" % m) for m in range(O_TILES)]
         kb_acc = [
             banks.tile([P, COLS], F32, name="kb_acc%d" % m, tag="bank%d" % (O_TILES + m))
             for m in range(O_TILES)
         ]
-        first = 0
-        for count in [CHUNK] * (CHUNKS - 1) + [1] * CHUNK:
-            wb_words = fetch_w(wb_passes, first, count)
-            project(nc, kb_acc, wb_words, wb_planes, x_codes, x_planes, first)
-            first += count
+        q_grouped = keep.tile([P, HALVES, V, PACK], BF16, align_bytes=64)
+        q_codes = keep.tile([P, HALVES, V], U32, align_bytes=64)
+        q_planes = keep.tile([P, HALVES, V], U8, align_bytes=64)
+
+        for step in range(PASSES + WB_LAG):
+            if step < PASSES:
+                if step + X_LEAD < PASSES:
+                    quantise_x(step + X_LEAD, fetch_x(step + X_LEAD))
+                wa_words = fetch_wa(step)
+                if step % CHUNK == 1 and step // CHUNK < WB_EARLY:
+                    load_scales_of_chunk(nc, wb_planes, Wb_scales, step // CHUNK)
+                if step % CHUNK == 2 and step // CHUNK + 1 < WA_EARLY:
+                    load_scales_of_chunk(nc, wa_planes, Wa_scales, step // CHUNK + 1)
+                project(nc, qa_acc, wa_words, wa_planes, x_codes, x_planes, step)
+                if step == PASSES - 1:
+                    leave_psum_and_quantise(
+                        nc, qa_acc, bias[:, 0:O_TILES], q_grouped, q_codes, q_planes
+                    )
+            if step >= WB_LAG:
+                wb_words = fetch_wb(step - WB_LAG)
+                project(nc, kb_acc, wb_words, wb_planes, x_codes, x_planes, step - WB_LAG)
 
         k_grouped = keep.tile([P, HALVES, V, PACK], BF16, align_bytes=64)
         k_codes = keep.tile([P, HALVES, V], U32, align_bytes=64)

@@ -32,10 +32,11 @@ RUN = 4
 FLOPS = 2 * 2 * IC * C * COLS + 2 * V * V * IC * T
 
 
-X_LEAD = 2
+PAIR = 2
+PAIRS = PASSES // PAIR
 WB_LAG = 4
-WA_EARLY = 6
-WB_EARLY = 2
+WA_EARLY = 3
+WB_EARLY = 5
 
 
 def load_scales_of_chunk(nc, planes, scales, c):
@@ -64,18 +65,20 @@ def regroup(copy, grouped, raw):
     )
 
 
-def project(nc, acc, w_words, w_planes, x_codes, x_planes, g):
+def project(nc, acc, w_words, w_planes, x_codes, x_planes, first):
     for m in (0, 2, 1, 3):
         o_cols = slice(m * P, (m + 1) * P)
-        nc.tensor.matmul_mx(
-            out=acc[m][:],
-            lhsT=w_words[:, o_cols].bitcast(FP8X4),
-            lhsT_scale=w_planes[4 * (g % CHUNK) : P, g // CHUNK, o_cols],
-            rhs=x_codes[:, g, :].bitcast(FP8X4),
-            rhs_scale=x_planes[:, g, :],
-            start=(g == 0),
-            stop=(g == PASSES - 1),
-        )
+        for i in range(w_words.shape[1]):
+            g = first + i
+            nc.tensor.matmul_mx(
+                out=acc[m][:],
+                lhsT=w_words[:, i, o_cols].bitcast(FP8X4),
+                lhsT_scale=w_planes[4 * (g % CHUNK) : P, g // CHUNK, o_cols],
+                rhs=x_codes[:, g, :].bitcast(FP8X4),
+                rhs_scale=x_planes[:, g, :],
+                start=(g == 0),
+                stop=(g == PASSES - 1),
+            )
 
 
 def leave_psum_and_quantise(nc, acc, bias, grouped, codes, planes):
@@ -99,15 +102,15 @@ def tile_adaptivegraphconstruction_k_kernel(
     tc, x, Wa_words, Wa_scales, ba, Wb_words, Wb_scales, bb, A, alpha, out
 ):
     nc = tc.nc
-    x_passes = x[0].rearrange("(g p j) t v -> g p (j t v)", p=P, j=PACK)
-    wa_passes = Wa_words.rearrange("g p n t -> g p (n t)")
-    wb_passes = Wb_words.rearrange("g p n t -> g p (n t)")
+    x_pairs = x[0].rearrange("(s i p j) t v -> s p i (j t v)", i=PAIR, p=P, j=PACK)
+    wa_passes = Wa_words.rearrange("g p n t -> p g (n t)")
+    wb_passes = Wb_words.rearrange("g p n t -> p g (n t)")
 
     with ExitStack() as stack:
         stack.enter_context(tc.manual_schedule())
         keep = stack.enter_context(tc.tile_pool(name="keep", bufs=1))
-        x_stage = stack.enter_context(tc.tile_pool(name="x_stage", bufs=6))
-        w_stage = stack.enter_context(tc.tile_pool(name="w_stage", bufs=20))
+        x_stage = stack.enter_context(tc.tile_pool(name="x_stage", bufs=4))
+        w_stage = stack.enter_context(tc.tile_pool(name="w_stage", bufs=10))
         banks = stack.enter_context(tc.psum_pool(name="banks", bufs=1))
 
         x_codes = keep.tile([P, PASSES, COLS], U32, align_bytes=64)
@@ -115,26 +118,32 @@ def tile_adaptivegraphconstruction_k_kernel(
         wa_planes = keep.tile([P, CHUNKS, IC], U8, align_bytes=64)
         wb_planes = keep.tile([P, CHUNKS, IC], U8, align_bytes=64)
 
-        def fetch_x(g):
-            raw = x_stage.tile([P, PACK * COLS], BF16)
-            nc.sync.dma_start(out=raw[:], in_=x_passes[g])
+        def fetch_x(s):
+            raw = x_stage.tile([P, PAIR, PACK * COLS], BF16)
+            nc.sync.dma_start(out=raw[:], in_=x_pairs[s])
             return raw
 
-        def quantise_x(g, raw):
-            grouped = x_stage.tile([P, COLS * PACK], BF16, align_bytes=64)
-            regroup(nc.scalar.copy, grouped[:], raw[:])
-            nc.vector.quantize_mx(
-                out=x_codes[:, g, :].bitcast(FP8X4), scales=x_planes[:, g, :], in_=grouped[:]
-            )
+        def quantise_x(s, raw):
+            grouped = x_stage.tile([P, PAIR, COLS * PACK], BF16, align_bytes=64)
+            for i in range(PAIR):
+                g = PAIR * s + i
+                regroup(nc.scalar.copy, grouped[:, i, :], raw[:, i, :])
+                nc.vector.quantize_mx(
+                    out=x_codes[:, g, :].bitcast(FP8X4), scales=x_planes[:, g, :], in_=grouped[:, i, :]
+                )
 
-        def fetch_wa(g):
-            wa_words = w_stage.tile([P, IC], U32, align_bytes=64)
-            nc.sync.dma_start(out=wa_words[:].bitcast(I32), in_=wa_passes[g].bitcast(I32))
+        def fetch_wa(first, count):
+            wa_words = w_stage.tile([P, count, IC], U32, align_bytes=64)
+            nc.sync.dma_start(
+                out=wa_words[:].bitcast(I32), in_=wa_passes[:, first : first + count, :].bitcast(I32)
+            )
             return wa_words
 
-        def fetch_wb(g):
-            wb_words = w_stage.tile([P, IC], U32, align_bytes=64)
-            nc.sync.dma_start(out=wb_words[:].bitcast(I32), in_=wb_passes[g].bitcast(I32))
+        def fetch_wb(first, count):
+            wb_words = w_stage.tile([P, count, IC], U32, align_bytes=64)
+            nc.sync.dma_start(
+                out=wb_words[:].bitcast(I32), in_=wb_passes[:, first : first + count, :].bitcast(I32)
+            )
             return wb_words
 
         bias_rows = keep.tile([P, P], BF16)
@@ -142,8 +151,8 @@ def tile_adaptivegraphconstruction_k_kernel(
         alpha_row = keep.tile([P, 2], BF16)
         nc.vector.memset(alpha_row[:], 0.0)
         nc.vector.memset(wa_planes[:, 0:1, :].bitcast(I32), 0)
-        nc.vector.memset(wb_planes[:].bitcast(I32), 0)
         nc.vector.memset(wa_planes[:, 1:CHUNKS, :].bitcast(I32), 0)
+        nc.vector.memset(wb_planes[:].bitcast(I32), 0)
         ones = keep.tile([P, P], BF16)
         nc.vector.memset(ones[:], 1.0)
         zero = keep.tile([P, 1], F32)
@@ -161,13 +170,11 @@ def tile_adaptivegraphconstruction_k_kernel(
 
         ident = keep.tile([P, P], BF16)
         make_identity(nc, ident[:])
-        load_later_scales(nc, wb_planes, Wb_scales, WB_EARLY)
         load_later_scales(nc, wa_planes, Wa_scales, WA_EARLY)
+        load_later_scales(nc, wb_planes, Wb_scales, WB_EARLY)
 
-        for g in range(X_LEAD):
-            quantise_x(g, fetch_x(g))
-            if g == 0:
-                load_scales_of_chunk(nc, wa_planes, Wa_scales, 0)
+        quantise_x(0, fetch_x(0))
+        load_scales_of_chunk(nc, wa_planes, Wa_scales, 0)
 
         bias_ps = banks.tile([P, P], BF16, tag="bank7")
         nc.tensor.transpose(bias_ps[:], bias_rows[:], ident[:])
@@ -187,23 +194,22 @@ def tile_adaptivegraphconstruction_k_kernel(
         q_codes = keep.tile([P, HALVES, V], U32, align_bytes=64)
         q_planes = keep.tile([P, HALVES, V], U8, align_bytes=64)
 
-        for step in range(PASSES + WB_LAG):
-            if step < PASSES:
-                if step + X_LEAD < PASSES:
-                    quantise_x(step + X_LEAD, fetch_x(step + X_LEAD))
-                wa_words = fetch_wa(step)
-                if step % CHUNK == 1 and step // CHUNK < WB_EARLY:
-                    load_scales_of_chunk(nc, wb_planes, Wb_scales, step // CHUNK)
-                if step % CHUNK == 2 and step // CHUNK + 1 < WA_EARLY:
-                    load_scales_of_chunk(nc, wa_planes, Wa_scales, step // CHUNK + 1)
-                project(nc, qa_acc, wa_words, wa_planes, x_codes, x_planes, step)
-                if step == PASSES - 1:
-                    leave_psum_and_quantise(
-                        nc, qa_acc, bias[:, 0:O_TILES], q_grouped, q_codes, q_planes
-                    )
-            if step >= WB_LAG:
-                wb_words = fetch_wb(step - WB_LAG)
-                project(nc, kb_acc, wb_words, wb_planes, x_codes, x_planes, step - WB_LAG)
+        for s in range(PAIRS):
+            if s + 1 < PAIRS:
+                quantise_x(s + 1, fetch_x(s + 1))
+            wa_words = fetch_wa(PAIR * s, PAIR)
+            if s % 2 == 0 and 1 <= s // 2 <= WB_EARLY:
+                load_scales_of_chunk(nc, wb_planes, Wb_scales, s // 2 - 1)
+            if s % 2 == 1 and s // 2 + 1 < WA_EARLY:
+                load_scales_of_chunk(nc, wa_planes, Wa_scales, s // 2 + 1)
+            project(nc, qa_acc, wa_words, wa_planes, x_codes, x_planes, PAIR * s)
+            if s >= WB_LAG:
+                wb_words = fetch_wb(PAIR * (s - WB_LAG), PAIR)
+                project(nc, kb_acc, wb_words, wb_planes, x_codes, x_planes, PAIR * (s - WB_LAG))
+        leave_psum_and_quantise(nc, qa_acc, bias[:, 0:O_TILES], q_grouped, q_codes, q_planes)
+        for g in range(PAIR * (PAIRS - WB_LAG), PASSES):
+            wb_words = fetch_wb(g, 1)
+            project(nc, kb_acc, wb_words, wb_planes, x_codes, x_planes, g)
 
         k_grouped = keep.tile([P, HALVES, V, PACK], BF16, align_bytes=64)
         k_codes = keep.tile([P, HALVES, V], U32, align_bytes=64)

from contextlib import ExitStack

import concourse.mybir as mybir
from concourse.masks import make_identity

F32 = mybir.dt.float32
BF16 = mybir.dt.bfloat16
I32 = mybir.dt.int32
U32 = mybir.dt.uint32
U8 = mybir.dt.uint8
FP8X4 = mybir.dt.float8_e4m3fn_x4
ACT = mybir.ActivationFunctionType
ALU = mybir.AluOpType
AXIS = mybir.AxisListType

P = 128
PACK = 4
K_PASS = P * PACK

C = 16384
T = 2
V = 128
IC = 512
COLS = T * V
PASSES = C // K_PASS
CHUNK = 4
CHUNKS = PASSES // CHUNK
O_TILES = IC // P
HALVES = (IC * T) // K_PASS
RUN = 4

FLOPS = 2 * 2 * IC * C * COLS + 2 * V * V * IC * T


PAIR = 2
PAIRS = PASSES // PAIR
WB_LAG = 4
WA_EARLY = 3
WB_EARLY = 5


def load_scales_of_chunk(nc, planes, scales, c):
    for quadrant in range(4):
        nc.sync.dma_start(
            out=planes[32 * quadrant : 32 * quadrant + 4 * CHUNK, c, :].bitcast(I32),
            in_=scales[CHUNK * c : CHUNK * (c + 1), 4 * quadrant : 4 * quadrant + 4, :].bitcast(I32),
        )


def load_later_scales(nc, planes, scales, c0):
    by_block = scales.rearrange("(c i) q n -> q i c n", i=CHUNK)
    for quadrant in range(4):
        for r in range(4):
            first = 32 * quadrant + r
            nc.gpsimd.dma_start(
                out=planes[first : first + 4 * CHUNK : 4, c0:, :].bitcast(F32),
                in_=by_block[4 * quadrant + r][:, c0:, :].bitcast(F32),
            )


def regroup(copy, grouped, raw):
    copy(
        out=grouped.rearrange("p (c i j) -> p c j i", i=RUN, j=PACK),
        in_=raw.rearrange("p (j c i) -> p c j i", j=PACK, i=RUN),
    )


def project(nc, acc, w_words, w_planes, x_codes, x_planes, first):
    for m in (0, 2, 1, 3):
        o_cols = slice(m * P, (m + 1) * P)
        for i in range(w_words.shape[1]):
            g = first + i
            nc.tensor.matmul_mx(
                out=acc[m][:],
                lhsT=w_words[:, i, o_cols].bitcast(FP8X4),
                lhsT_scale=w_planes[4 * (g % CHUNK) : P, g // CHUNK, o_cols],
                rhs=x_codes[:, g, :].bitcast(FP8X4),
                rhs_scale=x_planes[:, g, :],
                start=(g == 0),
                stop=(g == PASSES - 1),
            )


def leave_psum_and_quantise(nc, acc, bias, grouped, codes, planes):
    for m in range(O_TILES):
        h, u = divmod(m, 2)
        dst = grouped[:, h, :, 2 * u : 2 * u + 2]
        src = acc[m][:].rearrange("p (t v) -> p v t", t=T)
        if h == 0:
            nc.scalar.activation(out=dst, in_=src, func=ACT.Identity, bias=bias[:, m : m + 1])
        else:
            nc.vector.tensor_scalar_add(out=dst, in0=src, scalar1=bias[:, m : m + 1])
    for h in range(HALVES):
        nc.vector.quantize_mx(
            out=codes[:, h, :].bitcast(FP8X4),
            scales=planes[:, h, :],
            in_=grouped[:, h, :, :].rearrange("p v j -> p (v j)"),
        )


def tile_adaptivegraphconstruction_k_kernel(
    tc, x, Wa_words, Wa_scales, ba, Wb_words, Wb_scales, bb, A, alpha, out
):
    nc = tc.nc
    x_pairs = x[0].rearrange("(s i p j) t v -> s p i (j t v)", i=PAIR, p=P, j=PACK)
    wa_passes = Wa_words.rearrange("g p n t -> p g (n t)")
    wb_passes = Wb_words.rearrange("g p n t -> p g (n t)")

    with ExitStack() as stack:
        stack.enter_context(tc.manual_schedule())
        keep = stack.enter_context(tc.tile_pool(name="keep", bufs=1))
        x_stage = stack.enter_context(tc.tile_pool(name="x_stage", bufs=4))
        w_stage = stack.enter_context(tc.tile_pool(name="w_stage", bufs=10))
        banks = stack.enter_context(tc.psum_pool(name="banks", bufs=1))

        x_codes = keep.tile([P, PASSES, COLS], U32, align_bytes=64)
        x_planes = keep.tile([P, PASSES, COLS], U8, align_bytes=64)
        wa_planes = keep.tile([P, CHUNKS, IC], U8, align_bytes=64)
        wb_planes = keep.tile([P, CHUNKS, IC], U8, align_bytes=64)

        def fetch_x(s):
            raw = x_stage.tile([P, PAIR, PACK * COLS], BF16)
            nc.sync.dma_start(out=raw[:], in_=x_pairs[s])
            return raw

        def quantise_x(s, raw):
            grouped = x_stage.tile([P, PAIR, COLS * PACK], BF16, align_bytes=64)
            for i in range(PAIR):
                g = PAIR * s + i
                regroup(nc.scalar.copy, grouped[:, i, :], raw[:, i, :])
                nc.vector.quantize_mx(
                    out=x_codes[:, g, :].bitcast(FP8X4), scales=x_planes[:, g, :], in_=grouped[:, i, :]
                )

        def fetch_wa(first, count):
            wa_words = w_stage.tile([P, count, IC], U32, align_bytes=64)
            nc.sync.dma_start(
                out=wa_words[:].bitcast(I32), in_=wa_passes[:, first : first + count, :].bitcast(I32)
            )
            return wa_words

        def fetch_wb(first, count):
            wb_words = w_stage.tile([P, count, IC], U32, align_bytes=64)
            nc.sync.dma_start(
                out=wb_words[:].bitcast(I32), in_=wb_passes[:, first : first + count, :].bitcast(I32)
            )
            return wb_words

        bias_rows = keep.tile([P, P], BF16)
        nc.vector.memset(bias_rows[:], 0.0)
        alpha_row = keep.tile([P, 2], BF16)
        nc.vector.memset(alpha_row[:], 0.0)
        nc.vector.memset(wa_planes[:, 0:1, :].bitcast(I32), 0)
        nc.vector.memset(wa_planes[:, 1:CHUNKS, :].bitcast(I32), 0)
        nc.vector.memset(wb_planes[:].bitcast(I32), 0)
        ones = keep.tile([P, P], BF16)
        nc.vector.memset(ones[:], 1.0)
        zero = keep.tile([P, 1], F32)
        nc.vector.memset(zero[:], 0.0)

        nc.scalar.dma_start(out=bias_rows[0:O_TILES, :], in_=ba.rearrange("(m p) -> m p", p=P))
        nc.scalar.dma_start(
            out=bias_rows[O_TILES : 2 * O_TILES, :], in_=bb.rearrange("(m p) -> m p", p=P)
        )
        nc.scalar.dma_start(out=alpha_row[0:1, 0:1], in_=alpha.unsqueeze(0))
        a_sb = keep.tile([P, V], BF16)
        nc.scalar.dma_start(out=a_sb[:], in_=A[0])
        warm = keep.tile([P, 1], F32)
        nc.scalar.activation(out=warm[:], in_=zero[:], func=ACT.Tanh)

        ident = keep.tile([P, P], BF16)
        make_identity(nc, ident[:])
        load_later_scales(nc, wa_planes, Wa_scales, WA_EARLY)
        load_later_scales(nc, wb_planes, Wb_scales, WB_EARLY)

        quantise_x(0, fetch_x(0))
        load_scales_of_chunk(nc, wa_planes, Wa_scales, 0)

        bias_ps = banks.tile([P, P], BF16, tag="bank7")
        nc.tensor.transpose(bias_ps[:], bias_rows[:], ident[:])
        alpha_ps = banks.tile([P, 2], F32, tag="bank6")
        nc.tensor.matmul(alpha_ps[:], lhsT=ones[:], rhs=alpha_row[:], start=True, stop=True)
        bias = keep.tile([P, 2 * O_TILES], F32)
        nc.vector.tensor_copy(out=bias[:], in_=bias_ps[:, 0 : 2 * O_TILES])
        alpha_sb = keep.tile([P, 1], F32)
        nc.vector.tensor_copy(out=alpha_sb[:], in_=alpha_ps[:, 0:1])

        qa_acc = [banks.tile([P, COLS], F32, name="qa_acc%d" % m, tag="bank%d" % m) for m in range(O_TILES)]
        kb_acc = [
            banks.tile([P, COLS], F32, name="kb_acc%d" % m, tag="bank%d" % (O_TILES + m))
            for m in range(O_TILES)
        ]
        q_grouped = keep.tile([P, HALVES, V, PACK], BF16, align_bytes=64)
        q_codes = keep.tile([P, HALVES, V], U32, align_bytes=64)
        q_planes = keep.tile([P, HALVES, V], U8, align_bytes=64)

        for s in range(PAIRS):
            if s + 1 < PAIRS:
                quantise_x(s + 1, fetch_x(s + 1))
            wa_words = fetch_wa(PAIR * s, PAIR)
            if s % 2 == 0 and 1 <= s // 2 <= WB_EARLY:
                load_scales_of_chunk(nc, wb_planes, Wb_scales, s // 2 - 1)
            if s % 2 == 1 and s // 2 + 1 < WA_EARLY:
                load_scales_of_chunk(nc, wa_planes, Wa_scales, s // 2 + 1)
            project(nc, qa_acc, wa_words, wa_planes, x_codes, x_planes, PAIR * s)
            if s >= WB_LAG:
                wb_words = fetch_wb(PAIR * (s - WB_LAG), PAIR)
                project(nc, kb_acc, wb_words, wb_planes, x_codes, x_planes, PAIR * (s - WB_LAG))
        leave_psum_and_quantise(nc, qa_acc, bias[:, 0:O_TILES], q_grouped, q_codes, q_planes)
        for g in range(PAIR * (PAIRS - WB_LAG), PASSES):
            wb_words = fetch_wb(g, 1)
            project(nc, kb_acc, wb_words, wb_planes, x_codes, x_planes, g)

        k_grouped = keep.tile([P, HALVES, V, PACK], BF16, align_bytes=64)
        k_codes = keep.tile([P, HALVES, V], U32, align_bytes=64)
        k_planes = keep.tile([P, HALVES, V], U8, align_bytes=64)
        leave_psum_and_quantise(
            nc, kb_acc, bias[:, O_TILES : 2 * O_TILES], k_grouped, k_codes, k_planes
        )

        g_ps = banks.tile([P, V], F32, tag="bank0")
        for h in range(HALVES):
            nc.tensor.matmul_mx(
                out=g_ps[:],
                lhsT=q_codes[:, h, :].bitcast(FP8X4),
                lhsT_scale=q_planes[:, h, :],
                rhs=k_codes[:, h, :].bitcast(FP8X4),
                rhs_scale=k_planes[:, h, :],
                start=(h == 0),
                stop=(h == HALVES - 1),
            )
        graph_b = keep.tile([P, V], F32)
        nc.scalar.activation(out=graph_b[:], in_=g_ps[:], func=ACT.Tanh, scale=1.0 / (IC * T))
        z = keep.tile([P, V], F32)
        nc.vector.scalar_tensor_tensor(
            out=z[:], in0=graph_b[:], scalar=alpha_sb[:, 0:1], in1=a_sb[:], op0=ALU.mult, op1=ALU.add
        )
        neg_max = keep.tile([P, 1], F32)
        nc.vector.tensor_reduce(out=neg_max[:], in_=z[:], axis=AXIS.X, op=ALU.max, negate=True)
        e = keep.tile([P, V], F32)
        e_sum = keep.tile([P, 1], F32)
        nc.scalar.activation(
            out=e[:], in_=z[:], func=ACT.Exp, bias=neg_max[:, 0:1], accum_out=e_sum[:]
        )
        inv_sum = keep.tile([P, 1], F32)
        nc.vector.reciprocal(out=inv_sum[:], in_=e_sum[:])
        prob = keep.tile([P, V], F32)
        nc.vector.tensor_scalar_mul(out=prob[:], in0=e[:], scalar1=inv_sum[:, 0:1])
        nc.sync.dma_start(out=out[0], in_=prob[:])
